import numpy as np
import ml_dtypes


def mxq(x, axis, fmt="e4m3"):
    dtype, down = {"e4m3": (ml_dtypes.float8_e4m3fn, 7), "e5m2": (ml_dtypes.float8_e5m2, 14)}[fmt]
    v = np.moveaxis(np.asarray(x, np.float32).astype(ml_dtypes.bfloat16).astype(np.float64), axis, -1)
    blocks = v.reshape(v.shape[:-1] + (-1, 32))
    amax = np.abs(blocks).max(-1, keepdims=True)
    byte = np.maximum(np.where(amax > 0, np.frexp(amax)[1] - 1 + 127, 0) - down, 1)
    scale = np.exp2(byte - 127.0)
    codes = (blocks / scale).astype(np.float32).astype(dtype).astype(np.float64)
    return np.moveaxis((codes * scale).reshape(v.shape), -1, axis)


WIDE = False


def mx_kscale(k):
    if not WIDE:
        return np.ones(k)
    levels = np.array([10, -10, 5, -5, 0])
    if k % 512:
        return np.exp2(np.random.permutation(np.resize(levels, k // 32))).repeat(32)
    a = np.empty((k // 512, 16))
    for p in range(k // 512):
        a[p, :8] = np.random.permutation(np.resize(levels, 8))
        for g in range(8):
            far = levels[np.abs(levels - a[p, g]) >= 10]
            a[p, g + 8] = far[np.random.randint(len(far))]
    return np.exp2(a.ravel()).repeat(32)


BF16 = ml_dtypes.bfloat16


def bf(x):
    return np.asarray(x, np.float32).astype(BF16)


def f64(x):
    return np.asarray(x).astype(np.float64)


N, I0, O0, I1, O1, I2, O2, D0, D1, D2 = 1024, 512, 512, 256, 256, 128, 128, 1, 3, 5


def irrep_linear(x, w):
    return (x.transpose(2, 0, 1) @ w.transpose(2, 1, 0)).transpose(1, 2, 0)


def setup_inputs():
    s = mx_kscale(I0)
    return {"x0e": bf(np.random.standard_normal((N, I0, D0)) * s[None, :, None]),
            "x1o": bf(np.random.standard_normal((N, I1, D1))),
            "x2e": bf(np.random.standard_normal((N, I2, D2))),
            "w0e": bf(np.random.standard_normal((O0, I0, D0)) / np.sqrt(I0) / s[None, :, None]),
            "w1o": bf(np.random.standard_normal((O1, I1, D1)) / np.sqrt(I1)),
            "w2e": bf(np.random.standard_normal((O2, I2, D2)) / np.sqrt(I2)),
            "bias": bf(np.random.standard_normal(O0) * 0.5)}


def reference(x0e, x1o, x2e, w0e, w1o, w2e, bias):
    y0e = irrep_linear(mxq(f64(x0e), 1, "e4m3"), mxq(f64(w0e), 1, "e4m3")) + f64(bias)[None, :, None]
    y1o = irrep_linear(f64(x1o), f64(w1o))
    y2e = irrep_linear(f64(x2e), f64(w2e))
    n = x0e.shape[0]
    return np.concatenate([y0e.reshape(n, -1), y1o.reshape(n, -1), y2e.reshape(n, -1)], axis=-1)

@@ -1,0 +1,361 @@
+from contextlib import ExitStack
+
+import concourse.mybir as mybir
+from concourse.masks import make_identity
+
+FLOPS = 2 * 1024 * (512 * 512 + 3 * 256 * 256 + 5 * 128 * 128)
+
+BF16 = mybir.dt.bfloat16
+F32 = mybir.dt.float32
+I32 = mybir.dt.int32
+U32 = mybir.dt.uint32
+U8 = mybir.dt.uint8
+FP8X4 = mybir.dt.float8_e4m3fn_x4
+ADD = mybir.AluOpType.add
+MULT = mybir.AluOpType.mult
+
+P = 128
+NT = 8
+WIDTH = {0: 512, 1: 768, 2: 640}
+CHUNKS = {
+    0: ((0, 2), (2, 4), (4, 8)),
+    1: ((0, 1), (1, 2), (2, 4), (4, 8)),
+    2: ((0, 2), (2, 4), (4, 8)),
+}
+
+
+def tile_linearlayer_kernel(tc, x0e, x1o, x2e, w0e, w1o, w2e, bias, out):
+    nc = tc.nc
+    with ExitStack() as ctx:
+        ctx.enter_context(tc.manual_schedule())
+        keep = ctx.enter_context(tc.tile_pool(name="keep", bufs=1))
+        tp = ctx.enter_context(tc.psum_pool(name="tp", bufs=3))
+        acc = ctx.enter_context(tc.psum_pool(name="acc", bufs=5))
+
+        xv = {
+            0: x0e.rearrange("(p t) i d -> p t (i d)", t=NT),
+            1: x1o.rearrange("(p t) i d -> p t (i d)", t=NT),
+            2: x2e.rearrange("(p t) i d -> p t (i d)", t=NT),
+        }
+        outv = out.rearrange("(p t) c -> p t c", t=NT)
+
+        def evac(eng, dst, src):
+            if eng == "v":
+                nc.vector.tensor_copy(out=dst, in_=src)
+            else:
+                nc.scalar.copy(out=dst, in_=src)
+
+        ident_f = keep.tile([P, P], F32, name="ident_f")
+        make_identity(nc, ident_f[:])
+        ident_b = keep.tile([P, P], BF16, name="ident_b")
+        make_identity(nc, ident_b[:])
+        ones = keep.tile([P, P], BF16, name="ones")
+        nc.vector.memset(ones[:], 1.0)
+        brow = keep.tile([P, 512], BF16, name="brow")
+        nc.vector.memset(brow[:], 0.0)
+
+        where = {}
+        x_sb = {}
+        for kind in range(3):
+            for c, (lo, hi) in enumerate(CHUNKS[kind]):
+                for t in range(lo, hi):
+                    where[(kind, t)] = (c, t - lo, hi - lo)
+
+        def load_x(kind, c):
+            lo, hi = CHUNKS[kind][c]
+            a = keep.tile([P, (hi - lo) * WIDTH[kind]], BF16, name="x%d_sb%d" % (kind, c))
+            nc.sync.dma_start(out=a[:].rearrange("p (t c) -> p t c", t=hi - lo), in_=xv[kind][:, lo:hi, :])
+            x_sb[(kind, c)] = a
+
+        w1v = w1o.rearrange("(a p) i d -> a p (i d)", p=P)
+        w1_sb = []
+
+        def load_w1(a):
+            w = keep.tile([P, 768], BF16, name="w1_sb%d" % a)
+            nc.sync.dma_start(out=w[:], in_=w1v[a])
+            w1_sb.append(w)
+
+        w2_sb = keep.tile([P, 640], BF16, name="w2_sb")
+        w0_sb = keep.tile([P, 4 * 512], BF16, name="w0_sb")
+
+        def load_bias():
+            nc.sync.dma_start(out=brow[0:1, :], in_=bias.rearrange("(a o) -> a o", a=1))
+
+        def load_w2():
+            nc.sync.dma_start(out=w2_sb[:], in_=w2e.rearrange("o i d -> o (i d)"))
+
+        def load_w0():
+            nc.sync.dma_start(
+                out=w0_sb[:].rearrange("p (a c) -> p a c", a=4),
+                in_=w0e.rearrange("(a p) i d -> p a (i d)", p=P),
+            )
+
+        load_x(1, 0)
+        load_w1(0)
+        load_w1(1)
+        load_x(1, 1)
+        load_x(0, 0)
+        load_bias()
+        load_w2()
+        load_w0()
+        load_x(2, 0)
+        load_x(1, 2)
+        load_x(0, 1)
+        load_x(0, 2)
+        load_x(2, 1)
+        load_x(2, 2)
+        load_x(1, 3)
+
+        bias_bc = keep.tile([P, 512], F32, name="bias_bc")
+
+        def prep_bias():
+            pb = acc.tile([P, 512], F32, name="pb", tag="acc")
+            nc.tensor.matmul(out=pb[:], lhsT=ones[:], rhs=brow[:], start=True, stop=True)
+            evac("v", bias_bc[:], pb[:])
+
+        w2d = keep.tile([P, 640], BF16, name="w2d")
+        w2T = keep.tile([P, 5, P], BF16, name="w2T")
+
+        def sort_w2():
+            nc.gpsimd.tensor_scalar(
+                out=w2d[:].rearrange("p (m i) -> p m i", m=5),
+                in0=w2_sb[:].rearrange("p (i m) -> p m i", m=5),
+                scalar1=1.0, scalar2=0.0, op0=MULT, op1=ADD,
+            )
+
+        def prep_w2():
+            bk = tp.tile([P, 5, P], BF16, name="bk_w2", tag="tp")
+            for m in range(5):
+                nc.tensor.transpose(bk[:, m, :], w2d[:, m * P : (m + 1) * P], ident_b[:])
+            evac("s", w2T[:], bk[:])
+
+        w1Tb = []
+
+        def prep_w1(a):
+            w1w = w1_sb[a][:].bitcast(F32).rearrange("p (j r) -> p j r", r=3)
+            bk = tp.tile([P, 3, P], F32, name="bk_w1", tag="tp")
+            for r in range(3):
+                nc.tensor.transpose(bk[:, r, :], w1w[:, :, r], ident_f[:])
+            wt = keep.tile([P, 3 * P], F32, name="w1T%d" % a)
+            evac("s", wt[:].rearrange("p (r o) -> p r o", r=3), bk[:])
+            w1Tb.append(wt[:].bitcast(BF16).rearrange("p (r o e) -> p r o e", r=3, e=2))
+
+        gw = keep.tile([P, 2048], BF16, name="gw", align_bytes=64)
+        wq = keep.tile([P, 512], U32, name="wq", align_bytes=64)
+        ws = keep.tile([P, 512], U8, name="ws", align_bytes=64)
+
+        def prep_w0(b):
+            w0f = w0_sb[:].bitcast(F32)
+            gwf = gw[:].bitcast(F32).rearrange("p (o u) -> p o u", u=2)
+            bk = tp.tile([P, 2, 256], F32, name="bk_w0", tag="tp")
+            for aa in range(2):
+                for u in range(2):
+                    c0 = 256 * (2 * b + aa)
+                    nc.tensor.transpose(bk[:, u, aa * P : (aa + 1) * P], w0f[:, c0 + u : c0 + 256 : 2], ident_f[:])
+            evac("vs"[b], gwf[:, 256 * b : 256 * b + 256, :], bk[:].rearrange("p u o -> p o u"))
+
+        def quant_w0():
+            nc.vector.quantize_mx(out=wq[:].bitcast(FP8X4), scales=ws[:], in_=gw[:])
+
+        gx = {}
+        xq = {}
+        xs = {}
+        x1Tb = {}
+        x2T = {}
+        x2d = {}
+
+        def sort2(g):
+            c, k, n = where[(2, 2 * g)]
+            d = keep.tile([P, 2 * 640], BF16, name="x2d%d" % g)
+            nc.gpsimd.tensor_scalar(
+                out=d[:].rearrange("p (t m i) -> p t m i", t=2, m=5),
+                in0=x_sb[(2, c)][:, 640 * k : 640 * (k + 2)].rearrange("p (t i m) -> p t m i", t=2, m=5),
+                scalar1=1.0, scalar2=0.0, op0=MULT, op1=ADD,
+            )
+            x2d[g] = d
+
+        def flip0(g):
+            c, k, n = where[(0, 2 * g)]
+            xf = x_sb[(0, c)][:].bitcast(F32)
+            bk0 = tp.tile([P, 2, 256], F32, name="bk_x0", tag="tp")
+            for tt in range(2):
+                for u in range(2):
+                    c0 = 256 * (k + tt)
+                    nc.tensor.transpose(bk0[:, u, tt * P : (tt + 1) * P], xf[:, c0 + u : c0 + 256 : 2], ident_f[:])
+            a = keep.tile([P, 1024], BF16, name="gx%d" % g, align_bytes=64)
+            evac("v", a[:].bitcast(F32).rearrange("p (n u) -> p n u", u=2), bk0[:].rearrange("p u n -> p n u"))
+            gx[g] = a
+
+        def quant0(g):
+            q = keep.tile([P, 256], U32, name="xq%d" % g, align_bytes=64)
+            s = keep.tile([P, 256], U8, name="xs%d" % g, align_bytes=64)
+            nc.vector.quantize_mx(out=q[:].bitcast(FP8X4), scales=s[:], in_=gx[g][:])
+            xq[g] = q
+            xs[g] = s
+
+        def flip1(t, eng):
+            c, k, n = where[(1, t)]
+            xw = x_sb[(1, c)][:].bitcast(F32).rearrange("p (t j r) -> p t j r", t=n, r=3)
+            bk1 = tp.tile([P, 3, P], F32, name="bk_x1", tag="tp")
+            for r in range(3):
+                nc.tensor.transpose(bk1[:, r, :], xw[:, k, :, r], ident_f[:])
+            xt = keep.tile([P, 3 * P], F32, name="x1T%d" % t)
+            evac(eng, xt[:].rearrange("p (r n) -> p r n", r=3), bk1[:])
+            x1Tb[t] = xt[:].bitcast(BF16).rearrange("p (r n e) -> p r n e", r=3, e=2)
+
+        def flip2(t, eng):
+            g, tt = divmod(t, 2)
+            bk2 = tp.tile([P, 5, P], BF16, name="bk_x2", tag="tp")
+            for m in range(5):
+                c0 = 640 * tt + 128 * m
+                nc.tensor.transpose(bk2[:, m, :], x2d[g][:, c0 : c0 + P], ident_b[:])
+            x2t = keep.tile([P, 5, P], BF16, name="x2T%d" % t)
+            evac(eng, x2t[:], bk2[:])
+            x2T[t] = x2t
+
+        o_sbs = {}
+
+        def o_of(t):
+            if t not in o_sbs:
+                o_sbs[t] = keep.tile([P, 1920], F32, name="o_sb%d" % t)
+            return o_sbs[t]
+
+        def store(t, lo, hi):
+            nc.sync.dma_start(out=outv[:, t, lo:hi], in_=o_of(t)[:, lo:hi])
+
+        def mm1(t, h, eng):
+            o_sb = o_of(t)
+            py = acc.tile([P, 3, P], F32, name="py1", tag="acc")
+            for m in range(3):
+                for par in range(2):
+                    r, e = divmod(3 * par + m, 2)
+                    nc.tensor.matmul(
+                        out=py[:, m, :], lhsT=x1Tb[t][:, r, :, e], rhs=w1Tb[h][:, r, :, e],
+                        start=(par == 0), stop=(par == 1),
+                    )
+            c0 = 512 + 384 * h
+            evac(eng, o_sb[:, c0 : c0 + 384].rearrange("p (o m) -> p o m", m=3), py[:].rearrange("p m o -> p o m"))
+
+        def mm0(t):
+            o_sb = o_of(t)
+            g, tt = divmod(t, 2)
+            p0 = acc.tile([P, 512], F32, name="p0", tag="acc")
+            nc.tensor.matmul_mx(
+                out=p0[:],
+                lhsT=xq[g][:, tt * P : (tt + 1) * P].bitcast(FP8X4), lhsT_scale=xs[g][:, tt * P : (tt + 1) * P],
+                rhs=wq[:].bitcast(FP8X4), rhs_scale=ws[:],
+                start=True, stop=True,
+            )
+            nc.vector.tensor_tensor(out=o_sb[:, 0:512], in0=p0[:], in1=bias_bc[:], op=ADD)
+
+        def mm2(t, h, eng):
+            o_sb = o_of(t)
+            py = acc.tile([P, 5, 64], F32, name="py2", tag="acc")
+            for m in range(5):
+                nc.tensor.matmul(
+                    out=py[:, m, :], lhsT=x2T[t][:, m, :], rhs=w2T[:, m, 64 * h : 64 * h + 64],
+                    start=True, stop=True,
+                )
+            c0 = 1280 + 320 * h
+            evac(eng, o_sb[:, c0 : c0 + 320].rearrange("p (o m) -> p o m", m=5), py[:].rearrange("p m o -> p o m"))
+
+        sort_w2()
+        for g in range(NT // 2):
+            sort2(g)
+
+        flip1(0, "s")
+        prep_w1(0)
+        prep_w1(1)
+        flip1(1, "v")
+        flip0(0)
+        mm1(0, 0, "s")
+        mm1(0, 1, "v")
+        store(0, 512, 1280)
+        mm1(1, 0, "v")
+        prep_w2()
+        prep_w0(0)
+        prep_w0(1)
+        quant0(0)
+        prep_bias()
+        flip1(2, "s")
+        flip2(0, "s")
+        mm1(1, 1, "s")
+        store(1, 512, 1280)
+        quant_w0()
+        flip0(1)
+        flip0(2)
+        flip2(1, "s")
+        mm1(2, 0, "v")
+        mm1(2, 1, "s")
+        store(2, 512, 1280)
+        quant0(1)
+        mm0(0)
+        store(0, 0, 512)
+        mm2(0, 0, "s")
+        mm0(1)
+        store(1, 0, 512)
+        mm2(0, 1, "v")
+        store(0, 1280, 1920)
+        flip2(2, "s")
+        flip2(3, "v")
+        flip0(3)
+        mm2(1, 0, "s")
+        mm2(1, 1, "s")
+        store(1, 1280, 1920)
+        mm0(2)
+        store(2, 0, 512)
+        mm2(2, 0, "s")
+        quant0(2)
+        mm2(2, 1, "v")
+        store(2, 1280, 1920)
+        flip1(3, "s")
+        flip1(4, "s")
+        flip2(4, "v")
+        mm2(3, 0, "s")
+        mm2(3, 1, "s")
+        store(3, 1280, 1920)
+        mm0(3)
+        store(3, 0, 512)
+        mm0(4)
+        store(4, 0, 512)
+        quant0(3)
+        mm1(3, 0, "s")
+        mm1(3, 1, "s")
+        store(3, 512, 1280)
+        mm1(4, 0, "v")
+        mm0(5)
+        store(5, 0, 512)
+        mm1(4, 1, "s")
+        store(4, 512, 1280)
+        mm2(4, 0, "s")
+        flip2(5, "v")
+        flip1(5, "s")
+        flip1(6, "s")
+        mm2(4, 1, "v")
+        store(4, 1280, 1920)
+        mm2(5, 0, "s")
+        mm2(5, 1, "s")
+        store(5, 1280, 1920)
+        mm0(6)
+        store(6, 0, 512)
+        mm1(5, 0, "s")
+        mm0(7)
+        store(7, 0, 512)
+        mm1(5, 1, "s")
+        store(5, 512, 1280)
+        flip2(6, "v")
+        flip2(7, "v")
+        flip1(7, "v")
+        mm2(6, 0, "s")
+        mm2(6, 1, "v")
+        store(6, 1280, 1920)
+        mm2(7, 0, "v")
+        mm2(7, 1, "s")
+        store(7, 1280, 1920)
+        mm1(6, 0, "v")
+        mm1(6, 1, "v")
+        store(6, 512, 1280)
+        mm1(7, 0, "v")
+        store(7, 512, 896)
+        mm1(7, 1, "v")
+        store(7, 896, 1280)

@@ -18,7 +18,7 @@ P = 128
 NT = 8
 WIDTH = {0: 512, 1: 768, 2: 640}
 CHUNKS = {
-    0: ((0, 2), (2, 4), (4, 8)),
+    0: ((0, 2), (2, 8)),
     1: ((0, 1), (1, 2), (2, 4), (4, 8)),
     2: ((0, 2), (2, 4), (4, 8)),
 }
@@ -37,7 +37,8 @@ def tile_linearlayer_kernel(tc, x0e, x1o, x2e, w0e, w1o, w2e, bias, out):
             1: x1o.rearrange("(p t) i d -> p t (i d)", t=NT),
             2: x2e.rearrange("(p t) i d -> p t (i d)", t=NT),
         }
-        outv = out.rearrange("(p t) c -> p t c", t=NT)
+        outv = out.rearrange("(p t) c -> p (t c)", t=NT)
+        o_all = keep.tile([P, NT * 1920], F32, name="o_all")
 
         def evac(eng, dst, src):
             if eng == "v":
@@ -49,7 +50,7 @@ def tile_linearlayer_kernel(tc, x0e, x1o, x2e, w0e, w1o, w2e, bias, out):
         make_identity(nc, ident_f[:])
         ident_b = keep.tile([P, P], BF16, name="ident_b")
         make_identity(nc, ident_b[:])
-        ones = keep.tile([P, P], BF16, name="ones")
+        ones = keep.tile([P, 512], BF16, name="ones")
         nc.vector.memset(ones[:], 1.0)
         brow = keep.tile([P, 512], BF16, name="brow")
         nc.vector.memset(brow[:], 0.0)
@@ -85,10 +86,7 @@ def tile_linearlayer_kernel(tc, x0e, x1o, x2e, w0e, w1o, w2e, bias, out):
             nc.sync.dma_start(out=w2_sb[:], in_=w2e.rearrange("o i d -> o (i d)"))
 
         def load_w0():
-            nc.sync.dma_start(
-                out=w0_sb[:].rearrange("p (a c) -> p a c", a=4),
-                in_=w0e.rearrange("(a p) i d -> p a (i d)", p=P),
-            )
+            nc.sync.dma_start(out=w0_sb[:], in_=w0e.rearrange("(p a) i d -> p (a i d)", a=4))
 
         load_x(1, 0)
         load_w1(0)
@@ -101,16 +99,20 @@ def tile_linearlayer_kernel(tc, x0e, x1o, x2e, w0e, w1o, w2e, bias, out):
         load_x(2, 0)
         load_x(1, 2)
         load_x(0, 1)
-        load_x(0, 2)
         load_x(2, 1)
         load_x(2, 2)
         load_x(1, 3)
 
         bias_bc = keep.tile([P, 512], F32, name="bias_bc")
 
+        def warm_up():
+            for n in (512, 512, 256):
+                pw = acc.tile([P, n], F32, name="pw", tag="acc")
+                nc.tensor.matmul(out=pw[:], lhsT=ones[:, 0:P], rhs=ones[:, 0:n], start=True, stop=True)
+
         def prep_bias():
             pb = acc.tile([P, 512], F32, name="pb", tag="acc")
-            nc.tensor.matmul(out=pb[:], lhsT=ones[:], rhs=brow[:], start=True, stop=True)
+            nc.tensor.matmul(out=pb[:], lhsT=ones[:, 0:P], rhs=brow[:], start=True, stop=True)
             evac("v", bias_bc[:], pb[:])
 
         w2d = keep.tile([P, 640], BF16, name="w2d")
@@ -164,15 +166,15 @@ def tile_linearlayer_kernel(tc, x0e, x1o, x2e, w0e, w1o, w2e, bias, out):
         x2T = {}
         x2d = {}
 
-        def sort2(g):
-            c, k, n = where[(2, 2 * g)]
-            d = keep.tile([P, 2 * 640], BF16, name="x2d%d" % g)
+        def sort2(t):
+            c, k, n = where[(2, t)]
+            d = keep.tile([P, 640], BF16, name="x2d%d" % t)
             nc.gpsimd.tensor_scalar(
-                out=d[:].rearrange("p (t m i) -> p t m i", t=2, m=5),
-                in0=x_sb[(2, c)][:, 640 * k : 640 * (k + 2)].rearrange("p (t i m) -> p t m i", t=2, m=5),
+                out=d[:].rearrange("p (m i) -> p m i", m=5),
+                in0=x_sb[(2, c)][:, 640 * k : 640 * (k + 1)].rearrange("p (i m) -> p m i", m=5),
                 scalar1=1.0, scalar2=0.0, op0=MULT, op1=ADD,
             )
-            x2d[g] = d
+            x2d[t] = d
 
         def flip0(g):
             c, k, n = where[(0, 2 * g)]
@@ -204,27 +206,18 @@ def tile_linearlayer_kernel(tc, x0e, x1o, x2e, w0e, w1o, w2e, bias, out):
             x1Tb[t] = xt[:].bitcast(BF16).rearrange("p (r n e) -> p r n e", r=3, e=2)
 
         def flip2(t, eng):
-            g, tt = divmod(t, 2)
             bk2 = tp.tile([P, 5, P], BF16, name="bk_x2", tag="tp")
             for m in range(5):
-                c0 = 640 * tt + 128 * m
-                nc.tensor.transpose(bk2[:, m, :], x2d[g][:, c0 : c0 + P], ident_b[:])
+                nc.tensor.transpose(bk2[:, m, :], x2d[t][:, 128 * m : 128 * m + P], ident_b[:])
             x2t = keep.tile([P, 5, P], BF16, name="x2T%d" % t)
             evac(eng, x2t[:], bk2[:])
             x2T[t] = x2t
 
-        o_sbs = {}
-
-        def o_of(t):
-            if t not in o_sbs:
-                o_sbs[t] = keep.tile([P, 1920], F32, name="o_sb%d" % t)
-            return o_sbs[t]
-
         def store(t, lo, hi):
-            nc.sync.dma_start(out=outv[:, t, lo:hi], in_=o_of(t)[:, lo:hi])
+            lo, hi = t * 1920 + lo, t * 1920 + hi
+            nc.sync.dma_start(out=outv[:, lo:hi], in_=o_all[:, lo:hi])
 
         def mm1(t, h, eng):
-            o_sb = o_of(t)
             py = acc.tile([P, 3, P], F32, name="py1", tag="acc")
             for m in range(3):
                 for par in range(2):
@@ -233,11 +226,10 @@ def tile_linearlayer_kernel(tc, x0e, x1o, x2e, w0e, w1o, w2e, bias, out):
                         out=py[:, m, :], lhsT=x1Tb[t][:, r, :, e], rhs=w1Tb[h][:, r, :, e],
                         start=(par == 0), stop=(par == 1),
                     )
-            c0 = 512 + 384 * h
-            evac(eng, o_sb[:, c0 : c0 + 384].rearrange("p (o m) -> p o m", m=3), py[:].rearrange("p m o -> p o m"))
+            c0 = t * 1920 + 512 + 384 * h
+            evac(eng, o_all[:, c0 : c0 + 384].rearrange("p (o m) -> p o m", m=3), py[:].rearrange("p m o -> p o m"))
 
         def mm0(t):
-            o_sb = o_of(t)
             g, tt = divmod(t, 2)
             p0 = acc.tile([P, 512], F32, name="p0", tag="acc")
             nc.tensor.matmul_mx(
@@ -246,30 +238,35 @@ def tile_linearlayer_kernel(tc, x0e, x1o, x2e, w0e, w1o, w2e, bias, out):
                 rhs=wq[:].bitcast(FP8X4), rhs_scale=ws[:],
                 start=True, stop=True,
             )
-            nc.vector.tensor_tensor(out=o_sb[:, 0:512], in0=p0[:], in1=bias_bc[:], op=ADD)
+            c0 = t * 1920
+            nc.vector.tensor_tensor(
+                out=o_all[:, c0 : c0 + 512].rearrange("p (o a) -> p o a", a=4),
+                in0=p0[:].rearrange("p (a o) -> p o a", a=4),
+                in1=bias_bc[:].rearrange("p (o a) -> p o a", a=4), op=ADD,
+            )
 
         def mm2(t, h, eng):
-            o_sb = o_of(t)
             py = acc.tile([P, 5, 64], F32, name="py2", tag="acc")
             for m in range(5):
                 nc.tensor.matmul(
                     out=py[:, m, :], lhsT=x2T[t][:, m, :], rhs=w2T[:, m, 64 * h : 64 * h + 64],
                     start=True, stop=True,
                 )
-            c0 = 1280 + 320 * h
-            evac(eng, o_sb[:, c0 : c0 + 320].rearrange("p (o m) -> p o m", m=5), py[:].rearrange("p m o -> p o m"))
+            c0 = t * 1920 + 1280 + 320 * h
+            evac(eng, o_all[:, c0 : c0 + 320].rearrange("p (o m) -> p o m", m=5), py[:].rearrange("p m o -> p o m"))
 
         sort_w2()
-        for g in range(NT // 2):
-            sort2(g)
+        for t in range(NT):
+            sort2(t)
 
+        warm_up()
         flip1(0, "s")
         prep_w1(0)
         prep_w1(1)
         flip1(1, "v")
-        flip0(0)
         mm1(0, 0, "s")
         mm1(0, 1, "v")
+        flip0(0)
         store(0, 512, 1280)
         mm1(1, 0, "v")
         prep_w2()
@@ -293,17 +290,15 @@ def tile_linearlayer_kernel(tc, x0e, x1o, x2e, w0e, w1o, w2e, bias, out):
         store(0, 0, 512)
         mm2(0, 0, "s")
         mm0(1)
-        store(1, 0, 512)
         mm2(0, 1, "v")
-        store(0, 1280, 1920)
+        store(0, 1280, 1920 + 512)
         flip2(2, "s")
         flip2(3, "v")
         flip0(3)
         mm2(1, 0, "s")
         mm2(1, 1, "s")
-        store(1, 1280, 1920)
         mm0(2)
-        store(2, 0, 512)
+        store(1, 1280, 1920 + 512)
         mm2(2, 0, "s")
         quant0(2)
         mm2(2, 1, "v")
@@ -335,9 +330,8 @@ def tile_linearlayer_kernel(tc, x0e, x1o, x2e, w0e, w1o, w2e, bias, out):
         store(4, 1280, 1920)
         mm2(5, 0, "s")
         mm2(5, 1, "s")
-        store(5, 1280, 1920)
         mm0(6)
-        store(6, 0, 512)
+        store(5, 1280, 1920 + 512)
         mm1(5, 0, "s")
         mm0(7)
         store(7, 0, 512)

@@ -139,7 +139,7 @@ def tile_linearlayer_kernel(tc, x0e, x1o, x2e, w0e, w1o, w2e, bias, out):
             for r in range(3):
                 nc.tensor.transpose(bk[:, r, :], w1w[:, :, r], ident_f[:])
             wt = keep.tile([P, 3 * P], F32, name="w1T%d" % a)
-            evac("s", wt[:].rearrange("p (r o) -> p r o", r=3), bk[:])
+            evac("vs"[a], wt[:].rearrange("p (r o) -> p r o", r=3), bk[:])
             w1Tb.append(wt[:].bitcast(BF16).rearrange("p (r o e) -> p r o e", r=3, e=2))
 
         gw = keep.tile([P, 2048], BF16, name="gw", align_bytes=64)
@@ -268,21 +268,20 @@ def tile_linearlayer_kernel(tc, x0e, x1o, x2e, w0e, w1o, w2e, bias, out):
         mm1(0, 1, "v")
         flip0(0)
         store(0, 512, 1280)
-        mm1(1, 0, "v")
         prep_w2()
+        mm1(1, 0, "v")
         prep_w0(0)
+        prep_bias()
         prep_w0(1)
         quant0(0)
-        prep_bias()
         flip1(2, "s")
-        flip2(0, "s")
         mm1(1, 1, "s")
         store(1, 512, 1280)
+        flip2(0, "s")
         quant_w0()
         flip0(1)
-        flip0(2)
-        flip2(1, "s")
         mm1(2, 0, "v")
+        flip2(1, "s")
         mm1(2, 1, "s")
         store(2, 512, 1280)
         quant0(1)
@@ -293,6 +292,7 @@ def tile_linearlayer_kernel(tc, x0e, x1o, x2e, w0e, w1o, w2e, bias, out):
         mm2(0, 1, "v")
         store(0, 1280, 1920 + 512)
         flip2(2, "s")
+        flip0(2)
         flip2(3, "v")
         flip0(3)
         mm2(1, 0, "s")
@@ -346,10 +346,10 @@ def tile_linearlayer_kernel(tc, x0e, x1o, x2e, w0e, w1o, w2e, bias, out):
         mm2(7, 0, "v")
         mm2(7, 1, "s")
         store(7, 1280, 1920)
-        mm1(6, 0, "v")
+        mm1(6, 0, "s")
         mm1(6, 1, "v")
         store(6, 512, 1280)
-        mm1(7, 0, "v")
+        mm1(7, 0, "s")
         store(7, 512, 896)
         mm1(7, 1, "v")
         store(7, 896, 1280)

@@ -139,7 +139,7 @@ def tile_linearlayer_kernel(tc, x0e, x1o, x2e, w0e, w1o, w2e, bias, out):
             for r in range(3):
                 nc.tensor.transpose(bk[:, r, :], w1w[:, :, r], ident_f[:])
             wt = keep.tile([P, 3 * P], F32, name="w1T%d" % a)
-            evac("vs"[a], wt[:].rearrange("p (r o) -> p r o", r=3), bk[:])
+            evac("s", wt[:].rearrange("p (r o) -> p r o", r=3), bk[:])
             w1Tb.append(wt[:].bitcast(BF16).rearrange("p (r o e) -> p r o e", r=3, e=2))
 
         gw = keep.tile([P, 2048], BF16, name="gw", align_bytes=64)
@@ -292,9 +292,8 @@ def tile_linearlayer_kernel(tc, x0e, x1o, x2e, w0e, w1o, w2e, bias, out):
         mm2(0, 1, "v")
         store(0, 1280, 1920 + 512)
         flip2(2, "s")
-        flip0(2)
         flip2(3, "v")
-        flip0(3)
+        flip0(2)
         mm2(1, 0, "s")
         mm2(1, 1, "s")
         mm0(2)
@@ -308,16 +307,17 @@ def tile_linearlayer_kernel(tc, x0e, x1o, x2e, w0e, w1o, w2e, bias, out):
         flip2(4, "v")
         mm2(3, 0, "s")
         mm2(3, 1, "s")
+        flip0(3)
         store(3, 1280, 1920)
         mm0(3)
         store(3, 0, 512)
         mm0(4)
         store(4, 0, 512)
-        quant0(3)
         mm1(3, 0, "s")
         mm1(3, 1, "s")
         store(3, 512, 1280)
         mm1(4, 0, "v")
+        quant0(3)
         mm0(5)
         store(5, 0, 512)
         mm1(4, 1, "s")

@@ -176,14 +176,43 @@ def tile_linearlayer_kernel(tc, x0e, x1o, x2e, w0e, w1o, w2e, bias, out):
             )
             x2d[t] = d
 
+        x0d = {}
+        x1d = {}
+
+        def sort0(g, eng):
+            c, k, n = where[(0, 2 * g)]
+            d = keep.tile([P, 512], F32, name="x0d%d" % g)
+            src = x_sb[(0, c)][:].bitcast(F32)[:, 256 * k : 256 * (k + 2)]
+            evac(eng, d[:].rearrange("p (t u w) -> p t u w", t=2, u=2), src.rearrange("p (t w u) -> p t u w", t=2, u=2))
+            x0d[g] = d
+
+        def sort1(t, eng):
+            c, k, n = where[(1, t)]
+            if eng == "g":
+                d = keep.tile([P, 768], BF16, name="x1d%d" % t)
+                nc.gpsimd.tensor_scalar(
+                    out=d[:].rearrange("p (r j e) -> p r j e", r=3, e=2),
+                    in0=x_sb[(1, c)][:, 768 * k : 768 * (k + 1)].rearrange("p (j r e) -> p r j e", r=3, e=2),
+                    scalar1=1.0, scalar2=0.0, op0=MULT, op1=ADD,
+                )
+                x1d[t] = d[:].bitcast(F32)
+            else:
+                d = keep.tile([P, 384], F32, name="x1d%d" % t)
+                src = x_sb[(1, c)][:].bitcast(F32)[:, 384 * k : 384 * (k + 1)]
+                evac(eng, d[:].rearrange("p (r j) -> p r j", r=3), src.rearrange("p (j r) -> p r j", r=3))
+                x1d[t] = d
+
         def flip0(g):
             c, k, n = where[(0, 2 * g)]
-            xf = x_sb[(0, c)][:].bitcast(F32)
             bk0 = tp.tile([P, 2, 256], F32, name="bk_x0", tag="tp")
             for tt in range(2):
                 for u in range(2):
-                    c0 = 256 * (k + tt)
-                    nc.tensor.transpose(bk0[:, u, tt * P : (tt + 1) * P], xf[:, c0 + u : c0 + 256 : 2], ident_f[:])
+                    if g in x0d:
+                        words = x0d[g][:, 256 * tt + 128 * u : 256 * tt + 128 * (u + 1)]
+                    else:
+                        c0 = 256 * (k + tt)
+                        words = x_sb[(0, c)][:].bitcast(F32)[:, c0 + u : c0 + 256 : 2]
+                    nc.tensor.transpose(bk0[:, u, tt * P : (tt + 1) * P], words, ident_f[:])
             a = keep.tile([P, 1024], BF16, name="gx%d" % g, align_bytes=64)
             evac("v", a[:].bitcast(F32).rearrange("p (n u) -> p n u", u=2), bk0[:].rearrange("p u n -> p n u"))
             gx[g] = a
@@ -197,10 +226,13 @@ def tile_linearlayer_kernel(tc, x0e, x1o, x2e, w0e, w1o, w2e, bias, out):
 
         def flip1(t, eng):
             c, k, n = where[(1, t)]
-            xw = x_sb[(1, c)][:].bitcast(F32).rearrange("p (t j r) -> p t j r", t=n, r=3)
             bk1 = tp.tile([P, 3, P], F32, name="bk_x1", tag="tp")
             for r in range(3):
-                nc.tensor.transpose(bk1[:, r, :], xw[:, k, :, r], ident_f[:])
+                if t in x1d:
+                    words = x1d[t][:, 128 * r : 128 * (r + 1)]
+                else:
+                    words = x_sb[(1, c)][:].bitcast(F32)[:, 384 * k + r : 384 * (k + 1) : 3]
+                nc.tensor.transpose(bk1[:, r, :], words, ident_f[:])
             xt = keep.tile([P, 3 * P], F32, name="x1T%d" % t)
             evac(eng, xt[:].rearrange("p (r n) -> p r n", r=3), bk1[:])
             x1Tb[t] = xt[:].bitcast(BF16).rearrange("p (r n e) -> p r n e", r=3, e=2)
@@ -276,6 +308,7 @@ def tile_linearlayer_kernel(tc, x0e, x1o, x2e, w0e, w1o, w2e, bias, out):
         quant0(0)
         flip1(2, "s")
         mm1(1, 1, "s")
+        sort1(3, "s")
         store(1, 512, 1280)
         flip2(0, "s")
         quant_w0()
@@ -292,6 +325,7 @@ def tile_linearlayer_kernel(tc, x0e, x1o, x2e, w0e, w1o, w2e, bias, out):
         mm2(0, 1, "v")
         store(0, 1280, 1920 + 512)
         flip2(2, "s")
+        sort1(4, "s")
         flip2(3, "v")
         flip0(2)
         mm2(1, 0, "s")
@@ -303,23 +337,23 @@ def tile_linearlayer_kernel(tc, x0e, x1o, x2e, w0e, w1o, w2e, bias, out):
         mm2(2, 1, "v")
         store(2, 1280, 1920)
         flip1(3, "s")
-        flip1(4, "s")
+        flip1(4, "v")
         flip2(4, "v")
         mm2(3, 0, "s")
         mm2(3, 1, "s")
-        flip0(3)
-        store(3, 1280, 1920)
+        sort1(5, "s")
         mm0(3)
         store(3, 0, 512)
         mm0(4)
-        store(4, 0, 512)
+        store(3, 1280, 1920 + 512)
+        flip0(3)
         mm1(3, 0, "s")
         mm1(3, 1, "s")
+        sort1(6, "s")
         store(3, 512, 1280)
         mm1(4, 0, "v")
         quant0(3)
         mm0(5)
-        store(5, 0, 512)
         mm1(4, 1, "s")
         store(4, 512, 1280)
         mm2(4, 0, "s")
@@ -327,14 +361,13 @@ def tile_linearlayer_kernel(tc, x0e, x1o, x2e, w0e, w1o, w2e, bias, out):
         flip1(5, "s")
         flip1(6, "s")
         mm2(4, 1, "v")
-        store(4, 1280, 1920)
+        store(4, 1280, 1920 + 512)
         mm2(5, 0, "s")
         mm2(5, 1, "s")
         mm0(6)
         store(5, 1280, 1920 + 512)
         mm1(5, 0, "s")
         mm0(7)
-        store(7, 0, 512)
         mm1(5, 1, "s")
         store(5, 512, 1280)
         flip2(6, "v")
@@ -342,7 +375,7 @@ def tile_linearlayer_kernel(tc, x0e, x1o, x2e, w0e, w1o, w2e, bias, out):
         flip1(7, "v")
         mm2(6, 0, "s")
         mm2(6, 1, "v")
-        store(6, 1280, 1920)
+        store(6, 1280, 1920 + 512)
         mm2(7, 0, "v")
         mm2(7, 1, "s")
         store(7, 1280, 1920)
@@ -350,6 +383,5 @@ def tile_linearlayer_kernel(tc, x0e, x1o, x2e, w0e, w1o, w2e, bias, out):
         mm1(6, 1, "v")
         store(6, 512, 1280)
         mm1(7, 0, "s")
-        store(7, 512, 896)
         mm1(7, 1, "v")
-        store(7, 896, 1280)
+        store(7, 512, 1280)

from contextlib import ExitStack

import concourse.mybir as mybir
from concourse.masks import make_identity

FLOPS = 2 * 1024 * (512 * 512 + 3 * 256 * 256 + 5 * 128 * 128)

BF16 = mybir.dt.bfloat16
F32 = mybir.dt.float32
I32 = mybir.dt.int32
U32 = mybir.dt.uint32
U8 = mybir.dt.uint8
FP8X4 = mybir.dt.float8_e4m3fn_x4
ADD = mybir.AluOpType.add
MULT = mybir.AluOpType.mult

P = 128
NT = 8
WIDTH = {0: 512, 1: 768, 2: 640}
CHUNKS = {
    0: ((0, 2), (2, 8)),
    1: ((0, 1), (1, 2), (2, 4), (4, 8)),
    2: ((0, 2), (2, 4), (4, 8)),
}


def tile_linearlayer_kernel(tc, x0e, x1o, x2e, w0e, w1o, w2e, bias, out):
    nc = tc.nc
    with ExitStack() as ctx:
        ctx.enter_context(tc.manual_schedule())
        keep = ctx.enter_context(tc.tile_pool(name="keep", bufs=1))
        tp = ctx.enter_context(tc.psum_pool(name="tp", bufs=3))
        acc = ctx.enter_context(tc.psum_pool(name="acc", bufs=5))

        xv = {
            0: x0e.rearrange("(p t) i d -> p t (i d)", t=NT),
            1: x1o.rearrange("(p t) i d -> p t (i d)", t=NT),
            2: x2e.rearrange("(p t) i d -> p t (i d)", t=NT),
        }
        outv = out.rearrange("(p t) c -> p (t c)", t=NT)
        o_all = keep.tile([P, NT * 1920], F32, name="o_all")

        def evac(eng, dst, src):
            if eng == "v":
                nc.vector.tensor_copy(out=dst, in_=src)
            else:
                nc.scalar.copy(out=dst, in_=src)

        ident_f = keep.tile([P, P], F32, name="ident_f")
        make_identity(nc, ident_f[:])
        ident_b = keep.tile([P, P], BF16, name="ident_b")
        make_identity(nc, ident_b[:])
        ones = keep.tile([P, 512], BF16, name="ones")
        nc.vector.memset(ones[:], 1.0)
        brow = keep.tile([P, 512], BF16, name="brow")
        nc.vector.memset(brow[:], 0.0)

        where = {}
        x_sb = {}
        for kind in range(3):
            for c, (lo, hi) in enumerate(CHUNKS[kind]):
                for t in range(lo, hi):
                    where[(kind, t)] = (c, t - lo, hi - lo)

        def load_x(kind, c):
            lo, hi = CHUNKS[kind][c]
            a = keep.tile([P, (hi - lo) * WIDTH[kind]], BF16, name="x%d_sb%d" % (kind, c))
            nc.sync.dma_start(out=a[:].rearrange("p (t c) -> p t c", t=hi - lo), in_=xv[kind][:, lo:hi, :])
            x_sb[(kind, c)] = a

        w1v = w1o.rearrange("(a p) i d -> a p (i d)", p=P)
        w1_sb = []

        def load_w1(a):
            w = keep.tile([P, 768], BF16, name="w1_sb%d" % a)
            nc.sync.dma_start(out=w[:], in_=w1v[a])
            w1_sb.append(w)

        w2_sb = keep.tile([P, 640], BF16, name="w2_sb")
        w0_sb = keep.tile([P, 4 * 512], BF16, name="w0_sb")

        def load_bias():
            nc.sync.dma_start(out=brow[0:1, :], in_=bias.rearrange("(a o) -> a o", a=1))

        def load_w2():
            nc.sync.dma_start(out=w2_sb[:], in_=w2e.rearrange("o i d -> o (i d)"))

        def load_w0():
            nc.sync.dma_start(out=w0_sb[:], in_=w0e.rearrange("(p a) i d -> p (a i d)", a=4))

        load_x(1, 0)
        load_w1(0)
        load_w1(1)
        load_x(1, 1)
        load_x(0, 0)
        load_bias()
        load_w2()
        load_w0()
        load_x(2, 0)
        load_x(1, 2)
        load_x(0, 1)
        load_x(2, 1)
        load_x(2, 2)
        load_x(1, 3)

        bias_bc = keep.tile([P, 512], F32, name="bias_bc")

        def warm_up():
            for n in (512, 512, 256):
                pw = acc.tile([P, n], F32, name="pw", tag="acc")
                nc.tensor.matmul(out=pw[:], lhsT=ones[:, 0:P], rhs=ones[:, 0:n], start=True, stop=True)

        def prep_bias():
            pb = acc.tile([P, 512], F32, name="pb", tag="acc")
            nc.tensor.matmul(out=pb[:], lhsT=ones[:, 0:P], rhs=brow[:], start=True, stop=True)
            evac("v", bias_bc[:], pb[:])

        w2d = keep.tile([P, 640], BF16, name="w2d")
        w2T = keep.tile([P, 5, P], BF16, name="w2T")

        def sort_w2():
            nc.gpsimd.tensor_scalar(
                out=w2d[:].rearrange("p (m i) -> p m i", m=5),
                in0=w2_sb[:].rearrange("p (i m) -> p m i", m=5),
                scalar1=1.0, scalar2=0.0, op0=MULT, op1=ADD,
            )

        def prep_w2():
            bk = tp.tile([P, 5, P], BF16, name="bk_w2", tag="tp")
            for m in range(5):
                nc.tensor.transpose(bk[:, m, :], w2d[:, m * P : (m + 1) * P], ident_b[:])
            evac("s", w2T[:], bk[:])

        w1Tb = []

        def prep_w1(a):
            w1w = w1_sb[a][:].bitcast(F32).rearrange("p (j r) -> p j r", r=3)
            bk = tp.tile([P, 3, P], F32, name="bk_w1", tag="tp")
            for r in range(3):
                nc.tensor.transpose(bk[:, r, :], w1w[:, :, r], ident_f[:])
            wt = keep.tile([P, 3 * P], F32, name="w1T%d" % a)
            evac("s", wt[:].rearrange("p (r o) -> p r o", r=3), bk[:])
            w1Tb.append(wt[:].bitcast(BF16).rearrange("p (r o e) -> p r o e", r=3, e=2))

        gw = keep.tile([P, 2048], BF16, name="gw", align_bytes=64)
        wq = keep.tile([P, 512], U32, name="wq", align_bytes=64)
        ws = keep.tile([P, 512], U8, name="ws", align_bytes=64)

        def prep_w0(b):
            w0f = w0_sb[:].bitcast(F32)
            gwf = gw[:].bitcast(F32).rearrange("p (o u) -> p o u", u=2)
            bk = tp.tile([P, 2, 256], F32, name="bk_w0", tag="tp")
            for aa in range(2):
                for u in range(2):
                    c0 = 256 * (2 * b + aa)
                    nc.tensor.transpose(bk[:, u, aa * P : (aa + 1) * P], w0f[:, c0 + u : c0 + 256 : 2], ident_f[:])
            evac("vs"[b], gwf[:, 256 * b : 256 * b + 256, :], bk[:].rearrange("p u o -> p o u"))

        def quant_w0():
            nc.vector.quantize_mx(out=wq[:].bitcast(FP8X4), scales=ws[:], in_=gw[:])

        gx = {}
        xq = {}
        xs = {}
        x1Tb = {}
        x2T = {}
        x2d = {}

        def sort2(t):
            c, k, n = where[(2, t)]
            d = keep.tile([P, 640], BF16, name="x2d%d" % t)
            nc.gpsimd.tensor_scalar(
                out=d[:].rearrange("p (m i) -> p m i", m=5),
                in0=x_sb[(2, c)][:, 640 * k : 640 * (k + 1)].rearrange("p (i m) -> p m i", m=5),
                scalar1=1.0, scalar2=0.0, op0=MULT, op1=ADD,
            )
            x2d[t] = d

        x0d = {}
        x1d = {}

        def sort0(g, eng):
            c, k, n = where[(0, 2 * g)]
            d = keep.tile([P, 512], F32, name="x0d%d" % g)
            src = x_sb[(0, c)][:].bitcast(F32)[:, 256 * k : 256 * (k + 2)]
            evac(eng, d[:].rearrange("p (t u w) -> p t u w", t=2, u=2), src.rearrange("p (t w u) -> p t u w", t=2, u=2))
            x0d[g] = d

        def sort1(t, eng):
            c, k, n = where[(1, t)]
            if eng == "g":
                d = keep.tile([P, 768], BF16, name="x1d%d" % t)
                nc.gpsimd.tensor_scalar(
                    out=d[:].rearrange("p (r j e) -> p r j e", r=3, e=2),
                    in0=x_sb[(1, c)][:, 768 * k : 768 * (k + 1)].rearrange("p (j r e) -> p r j e", r=3, e=2),
                    scalar1=1.0, scalar2=0.0, op0=MULT, op1=ADD,
                )
                x1d[t] = d[:].bitcast(F32)
            else:
                d = keep.tile([P, 384], F32, name="x1d%d" % t)
                src = x_sb[(1, c)][:].bitcast(F32)[:, 384 * k : 384 * (k + 1)]
                evac(eng, d[:].rearrange("p (r j) -> p r j", r=3), src.rearrange("p (j r) -> p r j", r=3))
                x1d[t] = d

        def flip0(g):
            c, k, n = where[(0, 2 * g)]
            bk0 = tp.tile([P, 2, 256], F32, name="bk_x0", tag="tp")
            for tt in range(2):
                for u in range(2):
                    if g in x0d:
                        words = x0d[g][:, 256 * tt + 128 * u : 256 * tt + 128 * (u + 1)]
                    else:
                        c0 = 256 * (k + tt)
                        words = x_sb[(0, c)][:].bitcast(F32)[:, c0 + u : c0 + 256 : 2]
                    nc.tensor.transpose(bk0[:, u, tt * P : (tt + 1) * P], words, ident_f[:])
            a = keep.tile([P, 1024], BF16, name="gx%d" % g, align_bytes=64)
            evac("v", a[:].bitcast(F32).rearrange("p (n u) -> p n u", u=2), bk0[:].rearrange("p u n -> p n u"))
            gx[g] = a

        def quant0(g):
            q = keep.tile([P, 256], U32, name="xq%d" % g, align_bytes=64)
            s = keep.tile([P, 256], U8, name="xs%d" % g, align_bytes=64)
            nc.vector.quantize_mx(out=q[:].bitcast(FP8X4), scales=s[:], in_=gx[g][:])
            xq[g] = q
            xs[g] = s

        def flip1(t, eng):
            c, k, n = where[(1, t)]
            bk1 = tp.tile([P, 3, P], F32, name="bk_x1", tag="tp")
            for r in range(3):
                if t in x1d:
                    words = x1d[t][:, 128 * r : 128 * (r + 1)]
                else:
                    words = x_sb[(1, c)][:].bitcast(F32)[:, 384 * k + r : 384 * (k + 1) : 3]
                nc.tensor.transpose(bk1[:, r, :], words, ident_f[:])
            xt = keep.tile([P, 3 * P], F32, name="x1T%d" % t)
            evac(eng, xt[:].rearrange("p (r n) -> p r n", r=3), bk1[:])
            x1Tb[t] = xt[:].bitcast(BF16).rearrange("p (r n e) -> p r n e", r=3, e=2)

        def flip2(t, eng):
            bk2 = tp.tile([P, 5, P], BF16, name="bk_x2", tag="tp")
            for m in range(5):
                nc.tensor.transpose(bk2[:, m, :], x2d[t][:, 128 * m : 128 * m + P], ident_b[:])
            x2t = keep.tile([P, 5, P], BF16, name="x2T%d" % t)
            evac(eng, x2t[:], bk2[:])
            x2T[t] = x2t

        def store(t, lo, hi):
            lo, hi = t * 1920 + lo, t * 1920 + hi
            nc.sync.dma_start(out=outv[:, lo:hi], in_=o_all[:, lo:hi])

        def mm1(t, h, eng):
            py = acc.tile([P, 3, P], F32, name="py1", tag="acc")
            for m in range(3):
                for par in range(2):
                    r, e = divmod(3 * par + m, 2)
                    nc.tensor.matmul(
                        out=py[:, m, :], lhsT=x1Tb[t][:, r, :, e], rhs=w1Tb[h][:, r, :, e],
                        start=(par == 0), stop=(par == 1),
                    )
            c0 = t * 1920 + 512 + 384 * h
            evac(eng, o_all[:, c0 : c0 + 384].rearrange("p (o m) -> p o m", m=3), py[:].rearrange("p m o -> p o m"))

        def mm0(t):
            g, tt = divmod(t, 2)
            p0 = acc.tile([P, 512], F32, name="p0", tag="acc")
            nc.tensor.matmul_mx(
                out=p0[:],
                lhsT=xq[g][:, tt * P : (tt + 1) * P].bitcast(FP8X4), lhsT_scale=xs[g][:, tt * P : (tt + 1) * P],
                rhs=wq[:].bitcast(FP8X4), rhs_scale=ws[:],
                start=True, stop=True,
            )
            c0 = t * 1920
            nc.vector.tensor_tensor(
                out=o_all[:, c0 : c0 + 512].rearrange("p (o a) -> p o a", a=4),
                in0=p0[:].rearrange("p (a o) -> p o a", a=4),
                in1=bias_bc[:].rearrange("p (o a) -> p o a", a=4), op=ADD,
            )

        def mm2(t, h, eng):
            py = acc.tile([P, 5, 64], F32, name="py2", tag="acc")
            for m in range(5):
                nc.tensor.matmul(
                    out=py[:, m, :], lhsT=x2T[t][:, m, :], rhs=w2T[:, m, 64 * h : 64 * h + 64],
                    start=True, stop=True,
                )
            c0 = t * 1920 + 1280 + 320 * h
            evac(eng, o_all[:, c0 : c0 + 320].rearrange("p (o m) -> p o m", m=5), py[:].rearrange("p m o -> p o m"))

        sort_w2()
        for t in range(NT):
            sort2(t)

        warm_up()
        flip1(0, "s")
        prep_w1(0)
        prep_w1(1)
        flip1(1, "v")
        mm1(0, 0, "s")
        mm1(0, 1, "v")
        flip0(0)
        store(0, 512, 1280)
        prep_w2()
        mm1(1, 0, "v")
        prep_w0(0)
        prep_bias()
        prep_w0(1)
        quant0(0)
        flip1(2, "s")
        mm1(1, 1, "s")
        sort1(3, "s")
        store(1, 512, 1280)
        flip2(0, "s")
        quant_w0()
        flip0(1)
        mm1(2, 0, "v")
        flip2(1, "s")
        mm1(2, 1, "s")
        store(2, 512, 1280)
        quant0(1)
        mm0(0)
        store(0, 0, 512)
        mm2(0, 0, "s")
        mm0(1)
        mm2(0, 1, "v")
        store(0, 1280, 1920 + 512)
        flip2(2, "s")
        sort1(4, "s")
        flip2(3, "v")
        flip0(2)
        mm2(1, 0, "s")
        mm2(1, 1, "s")
        mm0(2)
        store(1, 1280, 1920 + 512)
        mm2(2, 0, "s")
        quant0(2)
        mm2(2, 1, "v")
        store(2, 1280, 1920)
        flip1(3, "s")
        flip1(4, "v")
        flip2(4, "v")
        mm2(3, 0, "s")
        mm2(3, 1, "s")
        sort1(5, "s")
        mm0(3)
        store(3, 0, 512)
        mm0(4)
        store(3, 1280, 1920 + 512)
        flip0(3)
        mm1(3, 0, "s")
        mm1(3, 1, "s")
        sort1(6, "s")
        store(3, 512, 1280)
        mm1(4, 0, "v")
        quant0(3)
        mm0(5)
        mm1(4, 1, "s")
        store(4, 512, 1280)
        mm2(4, 0, "s")
        flip2(5, "v")
        flip1(5, "s")
        flip1(6, "s")
        mm2(4, 1, "v")
        store(4, 1280, 1920 + 512)
        mm2(5, 0, "s")
        mm2(5, 1, "s")
        mm0(6)
        store(5, 1280, 1920 + 512)
        mm1(5, 0, "s")
        mm0(7)
        mm1(5, 1, "s")
        store(5, 512, 1280)
        flip2(6, "v")
        flip2(7, "v")
        flip1(7, "v")
        mm2(6, 0, "s")
        mm2(6, 1, "v")
        store(6, 1280, 1920 + 512)
        mm2(7, 0, "v")
        mm2(7, 1, "s")
        store(7, 1280, 1920)
        mm1(6, 0, "s")
        mm1(6, 1, "v")
        store(6, 512, 1280)
        mm1(7, 0, "s")
        mm1(7, 1, "v")
        store(7, 512, 1280)
